import numpy as np
import ml_dtypes


def mxq(x, axis, fmt="e4m3"):
    dtype, down = {"e4m3": (ml_dtypes.float8_e4m3fn, 7), "e5m2": (ml_dtypes.float8_e5m2, 14)}[fmt]
    v = np.moveaxis(np.asarray(x, np.float32).astype(ml_dtypes.bfloat16).astype(np.float64), axis, -1)
    blocks = v.reshape(v.shape[:-1] + (-1, 32))
    amax = np.abs(blocks).max(-1, keepdims=True)
    byte = np.maximum(np.where(amax > 0, np.frexp(amax)[1] - 1 + 127, 0) - down, 1)
    scale = np.exp2(byte - 127.0)
    codes = (blocks / scale).astype(np.float32).astype(dtype).astype(np.float64)
    return np.moveaxis((codes * scale).reshape(v.shape), -1, axis)


WIDE = False


def mx_kscale(k):
    if not WIDE:
        return np.ones(k)
    levels = np.array([10, -10, 5, -5, 0])
    a = np.random.permutation(np.resize(levels, k // 512 * 4)).reshape(k // 512, 4)
    idx = np.arange(k)
    return np.exp2(a[idx // 512, idx % 128 // 32])


BF16 = ml_dtypes.bfloat16


def bf(x):
    return np.asarray(x, np.float32).astype(BF16)


def f64(x):
    return np.asarray(x).astype(np.float64)


E2M1 = np.array([0.0, 0.5, 1.0, 1.5, 2.0, 3.0, 4.0, 6.0, -0.0, -0.5, -1.0, -1.5, -2.0, -3.0, -4.0, -6.0])


def pack_weight(w, fmt):
    k, n = w.shape
    w = f64(bf(w)).reshape(k // 32, 32, n)
    amax = np.abs(w).max(1)
    if fmt == "e4m3":
        byte = np.frexp(amax)[1] - 1 + 127 - 7
    else:
        mant, ex = np.frexp(amax / 6.0)
        byte = np.where(mant > 0.5, ex, ex - 1) + 127
    byte = np.clip(np.where(amax > 0, byte, 1), 1, 254)
    scaled = (w * np.exp2(127.0 - byte)[:, None, :]).reshape(k, n).astype(np.float32)
    by_word = np.ascontiguousarray(scaled.reshape(k // 512, 128, 4, n).transpose(0, 1, 3, 2))
    if fmt == "e4m3":
        words = by_word.astype(ml_dtypes.float8_e4m3fn).view(np.uint8)
    else:
        c = by_word.astype(ml_dtypes.float4_e2m1fn).view(np.uint8) & 0xF
        words = c[..., 0::2] | (c[..., 1::2] << 4)
    return np.ascontiguousarray(words), np.ascontiguousarray(byte.astype(np.uint8).reshape(k // 512, 16, n))


def unpack_weight(words, scales, fmt):
    g, p, n, _ = words.shape
    if fmt == "e4m3":
        vals = np.ascontiguousarray(words).view(ml_dtypes.float8_e4m3fn).astype(np.float64)
    else:
        nib = np.empty((g, p, n, 4), np.uint8)
        nib[..., 0::2] = words & 0xF
        nib[..., 1::2] = words >> 4
        vals = E2M1[nib]
    vals = vals * np.repeat(np.exp2(scales.astype(np.float64) - 127.0), 8, axis=1)[..., None]
    return vals.transpose(0, 1, 3, 2).reshape(g * 512, n)


B, S, D, H, DH, F = 4, 2048, 1024, 2, 64, 4096
E = H * DH
EPS = 1e-5
FMT = "e4m3"


def layernorm(x, g, b):
    mu = x.mean(-1, keepdims=True)
    var = np.square(x - mu).mean(-1, keepdims=True)
    return (x - mu) / np.sqrt(var + EPS) * g + b


def make_pe():
    position = np.arange(S)[:, None] * 1.0
    div_term = np.exp(np.arange(0, DH, 2) * -(np.log(10000.0) / DH))
    pe = np.zeros((S, DH))
    pe[:, 0::2] = np.sin(position * div_term)
    pe[:, 1::2] = np.cos(position * div_term)
    return pe


def rope(t, pe):
    tr = t.reshape(B, H, S, DH // 2, 2)
    c = pe[:S, 0::2][None, None]
    d = pe[:S, 1::2][None, None]
    t0 = tr[..., 0] * c - tr[..., 1] * d
    t1 = tr[..., 0] * d + tr[..., 1] * c
    return np.stack([t0, t1], axis=-1).reshape(B, H, S, DH)


def setup_inputs():
    s = mx_kscale(D)
    x = np.random.standard_normal((B, S, D)) + 0.5 * np.random.standard_normal((B, S, 1))
    w_qkv = np.random.standard_normal((3 * E, D)) / np.sqrt(D) / s
    words, scales = pack_weight(w_qkv.T, FMT)
    return {"x": bf(x),
            "pe": bf(make_pe()),
            "w_qkv_words": words,
            "w_qkv_scales": scales,
            "g1": bf((1.0 + 0.1 * np.random.standard_normal(D)) * s),
            "b1": bf(0.1 * np.random.standard_normal(D) * s)}


def reference(x, pe, w_qkv_words, w_qkv_scales, g1, b1):
    h = layernorm(f64(x), f64(g1), f64(b1))
    qkv = mxq(h, 2, "e4m3") @ unpack_weight(w_qkv_words, w_qkv_scales, FMT)
    qkv = qkv.reshape(B, S, 3, H, DH)
    q, k, v = [qkv[:, :, i].transpose(0, 2, 1, 3) for i in range(3)]
    p = f64(pe)
    return rope(q, p), rope(k, p), v

@@ -1,0 +1,284 @@
+from concourse import mybir
+from concourse.masks import make_identity
+
+F32 = mybir.dt.float32
+BF16 = mybir.dt.bfloat16
+I32 = mybir.dt.int32
+U32 = mybir.dt.uint32
+U8 = mybir.dt.uint8
+FP8X4 = mybir.dt.float8_e4m3fn_x4
+ACT = mybir.ActivationFunctionType
+ALU = mybir.AluOpType
+
+P = 128
+PACK = 4
+K_PASS = P * PACK
+
+BATCH, SEQ, D_MODEL, HEADS, D_HEAD = 4, 2048, 1024, 2, 64
+N_QK = 2 * HEADS * D_HEAD
+N_V = HEADS * D_HEAD
+N_OUT = N_QK + N_V
+PASSES = D_MODEL // K_PASS
+PLANES = PASSES * PACK
+EPS = 1e-5
+
+TILES = 4
+GROUP = TILES * P
+GROUPS = BATCH * SEQ // GROUP
+SEQ_BLOCKS = SEQ // GROUP
+BN_CHUNK = 512
+VECTOR_TILES = TILES - 1
+
+FLOPS = 2 * BATCH * SEQ * D_MODEL * N_OUT
+
+
+def tile_minitransformerlayer_pa_t_kernel(
+    tc, x, pe, w_qkv_words, w_qkv_scales, g1, b1, out_0, out_1, out_2
+):
+    nc = tc.nc
+    x_rows = x.flatten_outer_dims()
+    outs = (out_0, out_1, out_2)
+
+    with (
+        tc.tile_pool(name="const", bufs=1) as const,
+        tc.tile_pool(name="load", bufs=4) as load,
+        tc.tile_pool(name="small", bufs=4) as small,
+        tc.tile_pool(name="work", bufs=2) as work,
+        tc.tile_pool(name="result", bufs=3) as result,
+        tc.psum_pool(name="turned", bufs=4) as turned,
+        tc.psum_pool(name="prod_qk", bufs=2) as prod_qk,
+        tc.psum_pool(name="prod_v", bufs=2) as prod_v,
+    ):
+        def load_group(grp):
+            x_sb = load.tile([P, TILES, D_MODEL], BF16, name="x_sb")
+            nc.sync.dma_start(
+                out=x_sb[:].rearrange("p i k -> p (i k)"),
+                in_=x_rows[grp * GROUP : (grp + 1) * GROUP, :].rearrange("(p i) k -> p (i k)", i=TILES),
+            )
+            return x_sb
+
+        x_next = load_group(0)
+
+        ident = const.tile([P, P], F32)
+        make_identity(nc, ident[:])
+        eps_col = const.tile([P, 1], F32)
+        nc.vector.memset(eps_col[:], EPS)
+
+        w_codes = const.tile([P, PASSES, N_OUT], U32, align_bytes=64)
+        nc.sync.dma_start(
+            out=w_codes[:].bitcast(I32),
+            in_=w_qkv_words.rearrange("g p n t -> p g (n t)").bitcast(I32),
+        )
+        w_planes = const.tile([P, PASSES, N_OUT], U8, align_bytes=64)
+        nc.vector.memset(w_planes[:].bitcast(I32), 0)
+        for quad in range(4):
+            nc.sync.dma_start(
+                out=w_planes[32 * quad : 32 * quad + 4, :, :].bitcast(I32),
+                in_=w_qkv_scales[:, 4 * quad : 4 * quad + 4, :]
+                .rearrange("g r n -> r g n")
+                .bitcast(I32),
+            )
+
+        gain_bf = const.tile([P, PASSES, PACK], BF16)
+        bias_bf = const.tile([P, PASSES, PACK], BF16)
+        nc.sync.dma_start(out=gain_bf[:], in_=g1.rearrange("(g q j) -> q g j", g=PASSES, j=PACK))
+        nc.sync.dma_start(out=bias_bf[:], in_=b1.rearrange("(g q j) -> q g j", g=PASSES, j=PACK))
+        gain = const.tile([P, PLANES], F32)
+        bias = const.tile([P, PLANES], F32)
+        nc.vector.tensor_copy(out=gain[:], in_=gain_bf[:].rearrange("q g j -> q (g j)"))
+        nc.vector.tensor_copy(out=bias[:], in_=bias_bf[:].rearrange("q g j -> q (g j)"))
+
+        pe_bf = const.tile([P, SEQ_BLOCKS, TILES * D_HEAD], BF16)
+        nc.sync.dma_start(
+            out=pe_bf[:], in_=pe.rearrange("(sb p i) f -> p sb (i f)", sb=SEQ_BLOCKS, i=TILES)
+        )
+        pe_pairs = pe_bf[:].rearrange("p sb (n e) -> p (sb n) e", e=2)
+        n_pairs = SEQ_BLOCKS * TILES * D_HEAD // 2
+        even_twice = const.tile([P, SEQ_BLOCKS, TILES, D_HEAD], F32)
+        odd_plus = const.tile([P, SEQ_BLOCKS, TILES, D_HEAD // 2], F32)
+        odd_minus = const.tile([P, SEQ_BLOCKS, TILES, D_HEAD // 2], F32)
+        nc.vector.tensor_copy(
+            out=even_twice[:].rearrange("p sb i (j e) -> p (sb i j) e", e=2),
+            in_=pe_pairs[:, :, 0].unsqueeze(2).to_broadcast([P, n_pairs, 2]),
+        )
+        nc.vector.tensor_copy(
+            out=odd_plus[:].rearrange("p sb i j -> p (sb i j)"), in_=pe_pairs[:, :, 1]
+        )
+        nc.vector.tensor_scalar_mul(
+            out=odd_minus[:].rearrange("p sb i j -> p (sb i j)"), in0=pe_pairs[:, :, 1], scalar1=-1.0
+        )
+
+        for grp in range(GROUPS):
+            batch, sb = divmod(grp, SEQ_BLOCKS)
+            positions = slice(sb * GROUP, (sb + 1) * GROUP)
+            x_sb = x_next
+            if grp + 1 < GROUPS:
+                x_next = load_group(grp + 1)
+
+            stats = small.tile([P, VECTOR_TILES, D_MODEL // BN_CHUNK, 6], F32)
+            mean_var = small.tile([P, VECTOR_TILES, 2], F32)
+            for i in range(VECTOR_TILES):
+                for c in range(D_MODEL // BN_CHUNK):
+                    nc.vector.bn_stats(
+                        out=stats[:, i, c, :], in_=x_sb[:, i, c * BN_CHUNK : (c + 1) * BN_CHUNK]
+                    )
+                nc.vector.bn_aggr(
+                    out=mean_var[:, i, :], in_=stats[:, i, :, :].rearrange("p c s -> p (c s)")
+                )
+            neg_mean = small.tile([P, VECTOR_TILES], F32)
+            nc.vector.tensor_scalar_mul(out=neg_mean[:], in0=mean_var[:, :, 0], scalar1=-1.0)
+            last = VECTOR_TILES
+            unread_a = work.tile([P, D_MODEL], BF16)
+            unread_b = work.tile([P, D_MODEL], BF16)
+            total = small.tile([P, 1], F32)
+            nc.scalar.activation(
+                out=unread_a[:], in_=x_sb[:, last, :], func=ACT.Identity, accum_out=total[:]
+            )
+            neg_mean_last = small.tile([P, 1], F32)
+            nc.scalar.mul(out=neg_mean_last[:], in_=total[:], mul=-1.0 / D_MODEL)
+            squares = small.tile([P, 1], F32)
+            nc.scalar.activation(
+                out=unread_b[:],
+                in_=x_sb[:, last, :],
+                func=ACT.Square,
+                bias=neg_mean_last[:],
+                scale=1.0,
+                accum_out=squares[:],
+            )
+            std = small.tile([P, TILES], F32)
+            nc.scalar.activation(
+                out=std[:, 0:last], in_=mean_var[:, :, 1], func=ACT.Sqrt, bias=eps_col[:], scale=1.0
+            )
+            nc.scalar.activation(
+                out=std[:, last:TILES],
+                in_=squares[:],
+                func=ACT.Sqrt,
+                bias=eps_col[:],
+                scale=1.0 / D_MODEL,
+            )
+            rstd = small.tile([P, TILES], F32)
+            nc.vector.reciprocal(out=rstd[:], in_=std[:])
+            shift_last = small.tile([P, 1], F32)
+            nc.scalar.mul(out=shift_last[:], in_=neg_mean_last[:], mul=rstd[:, last:TILES])
+
+            normed = work.tile([P, TILES, PLANES, P], F32)
+            for i in range(VECTOR_TILES):
+                nc.gpsimd.tensor_scalar(
+                    out=normed[:, i, :, :].rearrange("p (g j) q -> p g j q", j=PACK),
+                    in0=x_sb[:, i, :].rearrange("p (g q j) -> p g j q", g=PASSES, j=PACK),
+                    scalar1=neg_mean[:, i : i + 1],
+                    scalar2=rstd[:, i : i + 1],
+                    op0=ALU.add,
+                    op1=ALU.mult,
+                )
+            nc.scalar.activation(
+                out=normed[:, last, :, :].rearrange("p (g j) q -> p g j q", j=PACK),
+                in_=x_sb[:, last, :].rearrange("p (g q j) -> p g j q", g=PASSES, j=PACK),
+                func=ACT.Identity,
+                bias=shift_last[:],
+                scale=rstd[:, last:TILES],
+            )
+
+            h_planes = work.tile([P, PLANES, GROUP], BF16)
+            for plane in range(PLANES):
+                bank = turned.tile([P, GROUP], F32)
+                for i in range(TILES):
+                    nc.tensor.transpose(
+                        out=bank[:, i * P : (i + 1) * P], in_=normed[:, i, plane, :], identity=ident[:]
+                    )
+                nc.scalar.activation(
+                    out=h_planes[:, plane, :],
+                    in_=bank[:],
+                    func=ACT.Identity,
+                    bias=bias[:, plane : plane + 1],
+                    scale=gain[:, plane : plane + 1],
+                )
+
+            grouped = work.tile([P, PASSES, GROUP * PACK], BF16, align_bytes=64)
+            h_codes = work.tile([P, PASSES, GROUP], U32, align_bytes=64)
+            h_scales = work.tile([P, PASSES, GROUP], U8, align_bytes=64)
+            for g in range(PASSES):
+                nc.vector.tensor_copy(
+                    out=grouped[:, g, :].rearrange("p (c r j) -> p c j r", r=4, j=PACK),
+                    in_=h_planes[:, g * PACK : (g + 1) * PACK, :].rearrange(
+                        "p j (c r) -> p c j r", r=4
+                    ),
+                )
+            for g in range(PASSES):
+                nc.vector.quantize_mx(
+                    out=h_codes[:, g, :].bitcast(FP8X4), scales=h_scales[:, g, :], in_=grouped[:, g, :]
+                )
+
+            res = result.tile([P, 3 * HEADS, TILES, D_HEAD], F32)
+            straight = work.tile([P, 2 * HEADS, TILES, D_HEAD], F32)
+            crossed = work.tile([P, 2 * HEADS, TILES, 2, D_HEAD // 2], F32)
+            acc_v = prod_v.tile([P, TILES, N_V], F32)
+            for half in range(TILES // 2):
+                acc_qk = prod_qk.tile([P, 2, N_QK], F32)
+                for ii in range(2):
+                    i = 2 * half + ii
+                    toks = slice(i * P, (i + 1) * P)
+                    for g in range(PASSES):
+                        nc.tensor.matmul_mx(
+                            out=acc_qk[:, ii, :],
+                            lhsT=h_codes[:, g, toks].bitcast(FP8X4),
+                            lhsT_scale=h_scales[:, g, toks],
+                            rhs=w_codes[:, g, 0:N_QK].bitcast(FP8X4),
+                            rhs_scale=w_planes[:, g, 0:N_QK],
+                            start=(g == 0),
+                            stop=(g == PASSES - 1),
+                        )
+                    for g in range(PASSES):
+                        nc.tensor.matmul_mx(
+                            out=acc_v[:, i, :],
+                            lhsT=h_codes[:, g, toks].bitcast(FP8X4),
+                            lhsT_scale=h_scales[:, g, toks],
+                            rhs=w_codes[:, g, N_QK:N_OUT].bitcast(FP8X4),
+                            rhs_scale=w_planes[:, g, N_QK:N_OUT],
+                            start=(g == 0),
+                            stop=(g == PASSES - 1),
+                        )
+
+                two = slice(2 * half, 2 * half + 2)
+                shape_f = [P, 2, 2 * HEADS, D_HEAD]
+                shape_j = [P, 2, 2 * HEADS, D_HEAD // 2]
+                pairs = acc_qk[:].rearrange("p ii (c j e) -> p ii c j e", c=2 * HEADS, e=2)
+                nc.vector.tensor_tensor(
+                    out=straight[:, :, two, :].rearrange("p c ii f -> p ii c f"),
+                    in0=acc_qk[:].rearrange("p ii (c f) -> p ii c f", c=2 * HEADS),
+                    in1=even_twice[:, sb, two, :].unsqueeze(2).to_broadcast(shape_f),
+                    op=ALU.mult,
+                )
+                nc.vector.tensor_tensor(
+                    out=crossed[:, :, two, 0, :].rearrange("p c ii j -> p ii c j"),
+                    in0=pairs[:, :, :, :, 1],
+                    in1=odd_minus[:, sb, two, :].unsqueeze(2).to_broadcast(shape_j),
+                    op=ALU.mult,
+                )
+                nc.vector.tensor_tensor(
+                    out=crossed[:, :, two, 1, :].rearrange("p c ii j -> p ii c j"),
+                    in0=pairs[:, :, :, :, 0],
+                    in1=odd_plus[:, sb, two, :].unsqueeze(2).to_broadcast(shape_j),
+                    op=ALU.mult,
+                )
+
+            nc.vector.tensor_tensor(
+                out=res[:, 0 : 2 * HEADS, :, :].rearrange("p c i (j e) -> p (c i) j e", e=2),
+                in0=straight[:].rearrange("p c i (j e) -> p (c i) j e", e=2),
+                in1=crossed[:].rearrange("p c i e j -> p (c i) j e"),
+                op=ALU.add,
+            )
+            nc.scalar.copy(
+                out=res[:, 2 * HEADS : 3 * HEADS, :, :].rearrange("p h i f -> p i h f"),
+                in_=acc_v[:].rearrange("p i (h f) -> p i h f", h=HEADS),
+            )
+
+            for which in range(3):
+                nc.sync.dma_start(
+                    out=outs[which][batch, :, positions, :].rearrange(
+                        "h (p i) f -> p h (i f)", i=TILES
+                    ),
+                    in_=res[:, which * HEADS : (which + 1) * HEADS, :, :].rearrange(
+                        "p h i f -> p h (i f)"
+                    ),
+                )

@@ -38,31 +38,42 @@ def tile_minitransformerlayer_pa_t_kernel(
     nc = tc.nc
     x_rows = x.flatten_outer_dims()
     outs = (out_0, out_1, out_2)
+    last = VECTOR_TILES
 
     with (
         tc.tile_pool(name="const", bufs=1) as const,
         tc.tile_pool(name="load", bufs=4) as load,
         tc.tile_pool(name="small", bufs=4) as small,
         tc.tile_pool(name="work", bufs=2) as work,
-        tc.tile_pool(name="result", bufs=3) as result,
+        tc.tile_pool(name="result", bufs=2) as result,
         tc.psum_pool(name="turned", bufs=4) as turned,
         tc.psum_pool(name="prod_qk", bufs=2) as prod_qk,
         tc.psum_pool(name="prod_v", bufs=2) as prod_v,
+        tc.manual_schedule(),
     ):
-        def load_group(grp):
-            x_sb = load.tile([P, TILES, D_MODEL], BF16, name="x_sb")
+        x_of, mean_var_of, neg_mean_of, neg_mean_last_of, squares_of = {}, {}, {}, {}, {}
+        std_of, rstd_of, normed_of, h_planes_of, h_words_of = {}, {}, {}, {}, {}
+        acc_of, products_of = {}, {}
+
+        def load_tokens(n):
+            if not 0 <= n < GROUPS:
+                return
+            x_sb = load.tile([P, TILES, D_MODEL], BF16)
             nc.sync.dma_start(
                 out=x_sb[:].rearrange("p i k -> p (i k)"),
-                in_=x_rows[grp * GROUP : (grp + 1) * GROUP, :].rearrange("(p i) k -> p (i k)", i=TILES),
+                in_=x_rows[n * GROUP : (n + 1) * GROUP, :].rearrange("(p i) k -> p (i k)", i=TILES),
             )
-            return x_sb
+            x_of[n] = x_sb
 
-        x_next = load_group(0)
+        load_tokens(0)
+        load_tokens(1)
 
-        ident = const.tile([P, P], F32)
-        make_identity(nc, ident[:])
         eps_col = const.tile([P, 1], F32)
         nc.vector.memset(eps_col[:], EPS)
+        sqrt_first = const.tile([P, 1], F32)
+        nc.scalar.activation(out=sqrt_first[:], in_=eps_col[:], func=ACT.Sqrt)
+        ident = const.tile([P, P], F32)
+        make_identity(nc, ident[:])
 
         w_codes = const.tile([P, PASSES, N_OUT], U32, align_bytes=64)
         nc.sync.dma_start(
@@ -85,8 +96,8 @@ def tile_minitransformerlayer_pa_t_kernel(
         nc.sync.dma_start(out=bias_bf[:], in_=b1.rearrange("(g q j) -> q g j", g=PASSES, j=PACK))
         gain = const.tile([P, PLANES], F32)
         bias = const.tile([P, PLANES], F32)
-        nc.vector.tensor_copy(out=gain[:], in_=gain_bf[:].rearrange("q g j -> q (g j)"))
-        nc.vector.tensor_copy(out=bias[:], in_=bias_bf[:].rearrange("q g j -> q (g j)"))
+        nc.gpsimd.tensor_copy(out=gain[:], in_=gain_bf[:].rearrange("q g j -> q (g j)"))
+        nc.gpsimd.tensor_copy(out=bias[:], in_=bias_bf[:].rearrange("q g j -> q (g j)"))
 
         pe_bf = const.tile([P, SEQ_BLOCKS, TILES * D_HEAD], BF16)
         nc.sync.dma_start(
@@ -97,24 +108,35 @@ def tile_minitransformerlayer_pa_t_kernel(
         even_twice = const.tile([P, SEQ_BLOCKS, TILES, D_HEAD], F32)
         odd_plus = const.tile([P, SEQ_BLOCKS, TILES, D_HEAD // 2], F32)
         odd_minus = const.tile([P, SEQ_BLOCKS, TILES, D_HEAD // 2], F32)
-        nc.vector.tensor_copy(
+        nc.gpsimd.tensor_scalar(
             out=even_twice[:].rearrange("p sb i (j e) -> p (sb i j) e", e=2),
-            in_=pe_pairs[:, :, 0].unsqueeze(2).to_broadcast([P, n_pairs, 2]),
+            in0=pe_pairs[:, :, 0].unsqueeze(2).to_broadcast([P, n_pairs, 2]),
+            scalar1=1.0,
+            scalar2=0.0,
+            op0=ALU.mult,
+            op1=ALU.add,
         )
-        nc.vector.tensor_copy(
-            out=odd_plus[:].rearrange("p sb i j -> p (sb i j)"), in_=pe_pairs[:, :, 1]
+        nc.gpsimd.tensor_scalar(
+            out=odd_plus[:].rearrange("p sb i j -> p (sb i j)"),
+            in0=pe_pairs[:, :, 1],
+            scalar1=1.0,
+            scalar2=0.0,
+            op0=ALU.mult,
+            op1=ALU.add,
         )
-        nc.vector.tensor_scalar_mul(
-            out=odd_minus[:].rearrange("p sb i j -> p (sb i j)"), in0=pe_pairs[:, :, 1], scalar1=-1.0
+        nc.gpsimd.tensor_scalar(
+            out=odd_minus[:].rearrange("p sb i j -> p (sb i j)"),
+            in0=pe_pairs[:, :, 1],
+            scalar1=-1.0,
+            scalar2=0.0,
+            op0=ALU.mult,
+            op1=ALU.add,
         )
 
-        for grp in range(GROUPS):
-            batch, sb = divmod(grp, SEQ_BLOCKS)
-            positions = slice(sb * GROUP, (sb + 1) * GROUP)
-            x_sb = x_next
-            if grp + 1 < GROUPS:
-                x_next = load_group(grp + 1)
-
+        def statistics_vector(n):
+            if not 0 <= n < GROUPS:
+                return
+            x_sb = x_of[n]
             stats = small.tile([P, VECTOR_TILES, D_MODEL // BN_CHUNK, 6], F32)
             mean_var = small.tile([P, VECTOR_TILES, 2], F32)
             for i in range(VECTOR_TILES):
@@ -127,7 +149,13 @@ def tile_minitransformerlayer_pa_t_kernel(
                 )
             neg_mean = small.tile([P, VECTOR_TILES], F32)
             nc.vector.tensor_scalar_mul(out=neg_mean[:], in0=mean_var[:, :, 0], scalar1=-1.0)
-            last = VECTOR_TILES
+            mean_var_of[n] = mean_var
+            neg_mean_of[n] = neg_mean
+
+        def statistics_scalar(n):
+            if not 0 <= n < GROUPS:
+                return
+            x_sb = x_of[n]
             unread_a = work.tile([P, D_MODEL], BF16)
             unread_b = work.tile([P, D_MODEL], BF16)
             total = small.tile([P, 1], F32)
@@ -145,46 +173,77 @@ def tile_minitransformerlayer_pa_t_kernel(
                 scale=1.0,
                 accum_out=squares[:],
             )
+            neg_mean_last_of[n] = neg_mean_last
+            squares_of[n] = squares
+
+        def roots(n):
+            if not 0 <= n < GROUPS:
+                return
             std = small.tile([P, TILES], F32)
             nc.scalar.activation(
-                out=std[:, 0:last], in_=mean_var[:, :, 1], func=ACT.Sqrt, bias=eps_col[:], scale=1.0
+                out=std[:, 0:last],
+                in_=mean_var_of[n][:, :, 1],
+                func=ACT.Sqrt,
+                bias=eps_col[:],
+                scale=1.0,
             )
             nc.scalar.activation(
                 out=std[:, last:TILES],
-                in_=squares[:],
+                in_=squares_of[n][:],
                 func=ACT.Sqrt,
                 bias=eps_col[:],
                 scale=1.0 / D_MODEL,
             )
-            rstd = small.tile([P, TILES], F32)
-            nc.vector.reciprocal(out=rstd[:], in_=std[:])
-            shift_last = small.tile([P, 1], F32)
-            nc.scalar.mul(out=shift_last[:], in_=neg_mean_last[:], mul=rstd[:, last:TILES])
+            std_of[n] = std
 
+        def reciprocals(n):
+            if not 0 <= n < GROUPS:
+                return
+            rstd = small.tile([P, TILES], F32)
+            nc.vector.reciprocal(out=rstd[:], in_=std_of[n][:])
+            rstd_of[n] = rstd
+
+        def normalise_gpsimd(n):
+            if not 0 <= n < GROUPS:
+                return
             normed = work.tile([P, TILES, PLANES, P], F32)
             for i in range(VECTOR_TILES):
                 nc.gpsimd.tensor_scalar(
                     out=normed[:, i, :, :].rearrange("p (g j) q -> p g j q", j=PACK),
-                    in0=x_sb[:, i, :].rearrange("p (g q j) -> p g j q", g=PASSES, j=PACK),
-                    scalar1=neg_mean[:, i : i + 1],
-                    scalar2=rstd[:, i : i + 1],
+                    in0=x_of[n][:, i, :].rearrange("p (g q j) -> p g j q", g=PASSES, j=PACK),
+                    scalar1=neg_mean_of[n][:, i : i + 1],
+                    scalar2=rstd_of[n][:, i : i + 1],
                     op0=ALU.add,
                     op1=ALU.mult,
                 )
+            normed_of[n] = normed
+
+        def normalise_scalar(n):
+            if not 0 <= n < GROUPS:
+                return
+            shift_last = small.tile([P, 1], F32)
+            nc.scalar.mul(
+                out=shift_last[:], in_=neg_mean_last_of[n][:], mul=rstd_of[n][:, last:TILES]
+            )
             nc.scalar.activation(
-                out=normed[:, last, :, :].rearrange("p (g j) q -> p g j q", j=PACK),
-                in_=x_sb[:, last, :].rearrange("p (g q j) -> p g j q", g=PASSES, j=PACK),
+                out=normed_of[n][:, last, :, :].rearrange("p (g j) q -> p g j q", j=PACK),
+                in_=x_of[n][:, last, :].rearrange("p (g q j) -> p g j q", g=PASSES, j=PACK),
                 func=ACT.Identity,
                 bias=shift_last[:],
-                scale=rstd[:, last:TILES],
+                scale=rstd_of[n][:, last:TILES],
             )
 
+        def turn(n):
+            if not 0 <= n < GROUPS:
+                return
             h_planes = work.tile([P, PLANES, GROUP], BF16)
             for plane in range(PLANES):
                 bank = turned.tile([P, GROUP], F32)
                 for i in range(TILES):
                     nc.tensor.transpose(
-                        out=bank[:, i * P : (i + 1) * P], in_=normed[:, i, plane, :], identity=ident[:]
+                        out=bank[:, i * P : (i + 1) * P],
+                        in_=normed_of[n][:, i, plane, :],
+                        identity=ident[:],
                     )
                 nc.scalar.activation(
                     out=h_planes[:, plane, :],
@@ -193,14 +252,18 @@ def tile_minitransformerlayer_pa_t_kernel(
                     bias=bias[:, plane : plane + 1],
                     scale=gain[:, plane : plane + 1],
                 )
+            h_planes_of[n] = h_planes
 
+        def quantise(n):
+            if not 0 <= n < GROUPS:
+                return
             grouped = work.tile([P, PASSES, GROUP * PACK], BF16, align_bytes=64)
             h_codes = work.tile([P, PASSES, GROUP], U32, align_bytes=64)
             h_scales = work.tile([P, PASSES, GROUP], U8, align_bytes=64)
             for g in range(PASSES):
                 nc.vector.tensor_copy(
                     out=grouped[:, g, :].rearrange("p (c r j) -> p c j r", r=4, j=PACK),
-                    in_=h_planes[:, g * PACK : (g + 1) * PACK, :].rearrange(
+                    in_=h_planes_of[n][:, g * PACK : (g + 1) * PACK, :].rearrange(
                         "p j (c r) -> p c j r", r=4
                     ),
                 )
@@ -208,13 +271,17 @@ def tile_minitransformerlayer_pa_t_kernel(
                 nc.vector.quantize_mx(
                     out=h_codes[:, g, :].bitcast(FP8X4), scales=h_scales[:, g, :], in_=grouped[:, g, :]
                 )
+            h_words_of[n] = (h_codes, h_scales)
 
-            res = result.tile([P, 3 * HEADS, TILES, D_HEAD], F32)
-            straight = work.tile([P, 2 * HEADS, TILES, D_HEAD], F32)
-            crossed = work.tile([P, 2 * HEADS, TILES, 2, D_HEAD // 2], F32)
+        def project(n):
+            if not 0 <= n < GROUPS:
+                return
+            h_codes, h_scales = h_words_of[n]
             acc_v = prod_v.tile([P, TILES, N_V], F32)
+            acc_halves = []
             for half in range(TILES // 2):
                 acc_qk = prod_qk.tile([P, 2, N_QK], F32)
+                acc_halves.append(acc_qk)
                 for ii in range(2):
                     i = 2 * half + ii
                     toks = slice(i * P, (i + 1) * P)
@@ -238,10 +305,20 @@ def tile_minitransformerlayer_pa_t_kernel(
                             start=(g == 0),
                             stop=(g == PASSES - 1),
                         )
+            acc_of[n] = (acc_halves, acc_v)
 
+        def rotate_products(n):
+            if not 0 <= n < GROUPS:
+                return
+            sb = n % SEQ_BLOCKS
+            acc_halves = acc_of[n][0]
+            straight = work.tile([P, 2 * HEADS, TILES, D_HEAD], F32)
+            crossed = work.tile([P, 2 * HEADS, TILES, 2, D_HEAD // 2], F32)
+            shape_f = [P, 2, 2 * HEADS, D_HEAD]
+            shape_j = [P, 2, 2 * HEADS, D_HEAD // 2]
+            for half in range(TILES // 2):
+                acc_qk = acc_halves[half]
                 two = slice(2 * half, 2 * half + 2)
-                shape_f = [P, 2, 2 * HEADS, D_HEAD]
-                shape_j = [P, 2, 2 * HEADS, D_HEAD // 2]
                 pairs = acc_qk[:].rearrange("p ii (c j e) -> p ii c j e", c=2 * HEADS, e=2)
                 nc.vector.tensor_tensor(
                     out=straight[:, :, two, :].rearrange("p c ii f -> p ii c f"),
@@ -261,7 +338,16 @@ def tile_minitransformerlayer_pa_t_kernel(
                     in1=odd_plus[:, sb, two, :].unsqueeze(2).to_broadcast(shape_j),
                     op=ALU.mult,
                 )
+            products_of[n] = (straight, crossed)
 
+        def combine_and_store(n):
+            if not 0 <= n < GROUPS:
+                return
+            batch, sb = divmod(n, SEQ_BLOCKS)
+            positions = slice(sb * GROUP, (sb + 1) * GROUP)
+            straight, crossed = products_of[n]
+            acc_v = acc_of[n][1]
+            res = result.tile([P, 3 * HEADS, TILES, D_HEAD], F32)
             nc.vector.tensor_tensor(
                 out=res[:, 0 : 2 * HEADS, :, :].rearrange("p c i (j e) -> p (c i) j e", e=2),
                 in0=straight[:].rearrange("p c i (j e) -> p (c i) j e", e=2),
@@ -272,7 +358,6 @@ def tile_minitransformerlayer_pa_t_kernel(
                 out=res[:, 2 * HEADS : 3 * HEADS, :, :].rearrange("p h i f -> p i h f"),
                 in_=acc_v[:].rearrange("p i (h f) -> p i h f", h=HEADS),
             )
-
             for which in range(3):
                 nc.sync.dma_start(
                     out=outs[which][batch, :, positions, :].rearrange(
@@ -282,3 +367,17 @@ def tile_minitransformerlayer_pa_t_kernel(
                         "p h i f -> p h (i f)"
                     ),
                 )
+
+        for t in range(GROUPS + 5):
+            load_tokens(t + 2)
+            roots(t - 1)
+            statistics_scalar(t)
+            quantise(t - 3)
+            combine_and_store(t - 5)
+            reciprocals(t - 1)
+            normalise_gpsimd(t - 1)
+            project(t - 4)
+            rotate_products(t - 4)
+            turn(t - 2)
+            normalise_scalar(t - 1)
+            statistics_vector(t)

@@ -348,7 +348,7 @@ def tile_minitransformerlayer_pa_t_kernel(
             straight, crossed = products_of[n]
             acc_v = acc_of[n][1]
             res = result.tile([P, 3 * HEADS, TILES, D_HEAD], F32)
-            nc.vector.tensor_tensor(
+            nc.gpsimd.tensor_tensor(
                 out=res[:, 0 : 2 * HEADS, :, :].rearrange("p c i (j e) -> p (c i) j e", e=2),
                 in0=straight[:].rearrange("p c i (j e) -> p (c i) j e", e=2),
                 in1=crossed[:].rearrange("p c i e j -> p (c i) j e"),
@@ -373,9 +373,9 @@ def tile_minitransformerlayer_pa_t_kernel(
             roots(t - 1)
             statistics_scalar(t)
             quantise(t - 3)
-            combine_and_store(t - 5)
             reciprocals(t - 1)
             normalise_gpsimd(t - 1)
+            combine_and_store(t - 5)
             project(t - 4)
             rotate_products(t - 4)
             turn(t - 2)

@@ -144,13 +144,11 @@ def tile_minitransformerlayer_pa_t_kernel(
                     nc.vector.bn_stats(
                         out=stats[:, i, c, :], in_=x_sb[:, i, c * BN_CHUNK : (c + 1) * BN_CHUNK]
                     )
+            for i in range(VECTOR_TILES):
                 nc.vector.bn_aggr(
                     out=mean_var[:, i, :], in_=stats[:, i, :, :].rearrange("p c s -> p (c s)")
                 )
-            neg_mean = small.tile([P, VECTOR_TILES], F32)
-            nc.vector.tensor_scalar_mul(out=neg_mean[:], in0=mean_var[:, :, 0], scalar1=-1.0)
             mean_var_of[n] = mean_var
-            neg_mean_of[n] = neg_mean
 
         def statistics_scalar(n):
             if not 0 <= n < GROUPS:
@@ -199,6 +197,9 @@ def tile_minitransformerlayer_pa_t_kernel(
         def reciprocals(n):
             if not 0 <= n < GROUPS:
                 return
+            neg_mean = small.tile([P, VECTOR_TILES], F32)
+            nc.vector.tensor_scalar_mul(out=neg_mean[:], in0=mean_var_of[n][:, :, 0], scalar1=-1.0)
+            neg_mean_of[n] = neg_mean
             rstd = small.tile([P, TILES], F32)
             nc.vector.reciprocal(out=rstd[:], in_=std_of[n][:])
             rstd_of[n] = rstd

@@ -28,6 +28,7 @@ GROUPS = BATCH * SEQ // GROUP
 SEQ_BLOCKS = SEQ // GROUP
 BN_CHUNK = 512
 VECTOR_TILES = TILES - 1
+SHARED = VECTOR_TILES - 1
 
 FLOPS = 2 * BATCH * SEQ * D_MODEL * N_OUT
 
@@ -59,10 +60,16 @@ def tile_minitransformerlayer_pa_t_kernel(
             if not 0 <= n < GROUPS:
                 return
             x_sb = load.tile([P, TILES, D_MODEL], BF16)
-            nc.sync.dma_start(
-                out=x_sb[:].rearrange("p i k -> p (i k)"),
-                in_=x_rows[n * GROUP : (n + 1) * GROUP, :].rearrange("(p i) k -> p (i k)", i=TILES),
-            )
+            rows = x_rows[n * GROUP : (n + 1) * GROUP, :]
+            if n == 0:
+                by_tile = rows.rearrange("(p i) k -> p i k", i=TILES)
+                for i in (0, last, 1, 2):
+                    nc.sync.dma_start(out=x_sb[:, i, :], in_=by_tile[:, i, :])
+            else:
+                nc.sync.dma_start(
+                    out=x_sb[:].rearrange("p i k -> p (i k)"),
+                    in_=rows.rearrange("(p i) k -> p (i k)", i=TILES),
+                )
             x_of[n] = x_sb
 
         load_tokens(0)
@@ -209,9 +216,12 @@ def tile_minitransformerlayer_pa_t_kernel(
                 return
             normed = work.tile([P, TILES, PLANES, P], F32)
             for i in range(VECTOR_TILES):
+                passes = 1 if i == SHARED else PASSES
                 nc.gpsimd.tensor_scalar(
-                    out=normed[:, i, :, :].rearrange("p (g j) q -> p g j q", j=PACK),
-                    in0=x_of[n][:, i, :].rearrange("p (g q j) -> p g j q", g=PASSES, j=PACK),
+                    out=normed[:, i, 0 : passes * PACK, :].rearrange("p (g j) q -> p g j q", j=PACK),
+                    in0=x_of[n][:, i, 0 : passes * K_PASS].rearrange(
+                        "p (g q j) -> p g j q", g=passes, j=PACK
+                    ),
                     scalar1=neg_mean_of[n][:, i : i + 1],
                     scalar2=rstd_of[n][:, i : i + 1],
                     op0=ALU.add,
@@ -223,8 +233,21 @@ def tile_minitransformerlayer_pa_t_kernel(
             if not 0 <= n < GROUPS:
                 return
             shift_last = small.tile([P, 1], F32)
+            shift_shared = small.tile([P, 1], F32)
             nc.scalar.mul(
                 out=shift_last[:], in_=neg_mean_last_of[n][:], mul=rstd_of[n][:, last:TILES]
+            )
+            nc.scalar.mul(
+                out=shift_shared[:],
+                in_=neg_mean_of[n][:, SHARED : SHARED + 1],
+                mul=rstd_of[n][:, SHARED : SHARED + 1],
+            )
+            nc.scalar.activation(
+                out=normed_of[n][:, SHARED, PACK:PLANES, :],
+                in_=x_of[n][:, SHARED, K_PASS:D_MODEL].rearrange("p (q j) -> p j q", j=PACK),
+                func=ACT.Identity,
+                bias=shift_shared[:],
+                scale=rstd_of[n][:, SHARED : SHARED + 1],
             )
             nc.scalar.activation(
                 out=normed_of[n][:, last, :, :].rearrange("p (g j) q -> p g j q", j=PACK),
@@ -349,17 +372,29 @@ def tile_minitransformerlayer_pa_t_kernel(
             straight, crossed = products_of[n]
             acc_v = acc_of[n][1]
             res = result.tile([P, 3 * HEADS, TILES, D_HEAD], F32)
-            nc.gpsimd.tensor_tensor(
-                out=res[:, 0 : 2 * HEADS, :, :].rearrange("p c i (j e) -> p (c i) j e", e=2),
-                in0=straight[:].rearrange("p c i (j e) -> p (c i) j e", e=2),
-                in1=crossed[:].rearrange("p c i e j -> p (c i) j e"),
-                op=ALU.add,
-            )
             nc.scalar.copy(
                 out=res[:, 2 * HEADS : 3 * HEADS, :, :].rearrange("p h i f -> p i h f"),
                 in_=acc_v[:].rearrange("p i (h f) -> p i h f", h=HEADS),
             )
-            for which in range(3):
+            if n < GROUPS - 1:
+                nc.gpsimd.tensor_tensor(
+                    out=res[:, 0 : 2 * HEADS, :, :].rearrange("p c i (j e) -> p (c i) j e", e=2),
+                    in0=straight[:].rearrange("p c i (j e) -> p (c i) j e", e=2),
+                    in1=crossed[:].rearrange("p c i e j -> p (c i) j e"),
+                    op=ALU.add,
+                )
+                order = (0, 1, 2)
+            else:
+                for which in range(2):
+                    heads = slice(which * HEADS, (which + 1) * HEADS)
+                    nc.vector.tensor_tensor(
+                        out=res[:, heads, :, :].rearrange("p c i (j e) -> p (c i) j e", e=2),
+                        in0=straight[:, heads, :, :].rearrange("p c i (j e) -> p (c i) j e", e=2),
+                        in1=crossed[:, heads, :, :, :].rearrange("p c i e j -> p (c i) j e"),
+                        op=ALU.add,
+                    )
+                order = (2, 0, 1)
+            for which in order:
                 nc.sync.dma_start(
                     out=outs[which][batch, :, positions, :].rearrange(
                         "h (p i) f -> p h (i f)", i=TILES

@@ -54,7 +54,7 @@ def tile_minitransformerlayer_pa_t_kernel(
     ):
         x_of, mean_var_of, neg_mean_of, neg_mean_last_of, squares_of = {}, {}, {}, {}, {}
         std_of, rstd_of, normed_of, h_planes_of, h_words_of = {}, {}, {}, {}, {}
-        acc_of, products_of = {}, {}
+        acc_of, products_of, shift_of = {}, {}, {}
 
         def load_tokens(n):
             if not 0 <= n < GROUPS:
@@ -113,8 +113,7 @@ def tile_minitransformerlayer_pa_t_kernel(
         pe_pairs = pe_bf[:].rearrange("p sb (n e) -> p (sb n) e", e=2)
         n_pairs = SEQ_BLOCKS * TILES * D_HEAD // 2
         even_twice = const.tile([P, SEQ_BLOCKS, TILES, D_HEAD], F32)
-        odd_plus = const.tile([P, SEQ_BLOCKS, TILES, D_HEAD // 2], F32)
-        odd_minus = const.tile([P, SEQ_BLOCKS, TILES, D_HEAD // 2], F32)
+        odd_signed = const.tile([P, SEQ_BLOCKS, TILES, D_HEAD], F32)
         nc.gpsimd.tensor_scalar(
             out=even_twice[:].rearrange("p sb i (j e) -> p (sb i j) e", e=2),
             in0=pe_pairs[:, :, 0].unsqueeze(2).to_broadcast([P, n_pairs, 2]),
@@ -123,22 +122,15 @@ def tile_minitransformerlayer_pa_t_kernel(
             op0=ALU.mult,
             op1=ALU.add,
         )
-        nc.gpsimd.tensor_scalar(
-            out=odd_plus[:].rearrange("p sb i j -> p (sb i j)"),
-            in0=pe_pairs[:, :, 1],
-            scalar1=1.0,
-            scalar2=0.0,
-            op0=ALU.mult,
-            op1=ALU.add,
-        )
-        nc.gpsimd.tensor_scalar(
-            out=odd_minus[:].rearrange("p sb i j -> p (sb i j)"),
-            in0=pe_pairs[:, :, 1],
-            scalar1=-1.0,
-            scalar2=0.0,
-            op0=ALU.mult,
-            op1=ALU.add,
-        )
+        for e, sign in ((0, -1.0), (1, 1.0)):
+            nc.gpsimd.tensor_scalar(
+                out=odd_signed[:].rearrange("p sb i (j e) -> p (sb i j) e", e=2)[:, :, e],
+                in0=pe_pairs[:, :, 1],
+                scalar1=sign,
+                scalar2=0.0,
+                op0=ALU.mult,
+                op1=ALU.add,
+            )
 
         def statistics_vector(n):
             if not 0 <= n < GROUPS:
@@ -162,13 +154,22 @@ def tile_minitransformerlayer_pa_t_kernel(
                 return
             x_sb = x_of[n]
             unread_a = work.tile([P, D_MODEL], BF16)
-            unread_b = work.tile([P, D_MODEL], BF16)
-            total = small.tile([P, 1], F32)
-            nc.scalar.activation(
-                out=unread_a[:], in_=x_sb[:, last, :], func=ACT.Identity, accum_out=total[:]
-            )
             neg_mean_last = small.tile([P, 1], F32)
-            nc.scalar.mul(out=neg_mean_last[:], in_=total[:], mul=-1.0 / D_MODEL)
+            nc.scalar.activation(
+                out=unread_a[:],
+                in_=x_sb[:, last, :],
+                func=ACT.Identity,
+                scale=-1.0 / D_MODEL,
+                accum_out=neg_mean_last[:],
+            )
+            neg_mean_last_of[n] = neg_mean_last
+
+        def squares_scalar(n):
+            if not 0 <= n < GROUPS:
+                return
+            x_sb = x_of[n]
+            neg_mean_last = neg_mean_last_of[n]
+            unread_b = work.tile([P, D_MODEL], BF16)
             squares = small.tile([P, 1], F32)
             nc.scalar.activation(
                 out=unread_b[:],
@@ -178,7 +179,6 @@ def tile_minitransformerlayer_pa_t_kernel(
                 scale=1.0,
                 accum_out=squares[:],
             )
-            neg_mean_last_of[n] = neg_mean_last
             squares_of[n] = squares
 
         def roots(n):
@@ -229,7 +229,7 @@ def tile_minitransformerlayer_pa_t_kernel(
                 )
             normed_of[n] = normed
 
-        def normalise_scalar(n):
+        def shifts_scalar(n):
             if not 0 <= n < GROUPS:
                 return
             shift_last = small.tile([P, 1], F32)
@@ -242,6 +242,12 @@ def tile_minitransformerlayer_pa_t_kernel(
                 in_=neg_mean_of[n][:, SHARED : SHARED + 1],
                 mul=rstd_of[n][:, SHARED : SHARED + 1],
             )
+            shift_of[n] = (shift_last, shift_shared)
+
+        def normalise_scalar(n):
+            if not 0 <= n < GROUPS:
+                return
+            shift_last, shift_shared = shift_of[n]
             nc.scalar.activation(
                 out=normed_of[n][:, SHARED, PACK:PLANES, :],
                 in_=x_of[n][:, SHARED, K_PASS:D_MODEL].rearrange("p (q j) -> p j q", j=PACK),
@@ -257,11 +263,14 @@ def tile_minitransformerlayer_pa_t_kernel(
                 scale=rstd_of[n][:, last:TILES],
             )
 
-        def turn(n):
+        def turn(n, first, behind):
             if not 0 <= n < GROUPS:
                 return
-            h_planes = work.tile([P, PLANES, GROUP], BF16)
-            for plane in range(PLANES):
+            if first == 0:
+                h_planes_new = work.tile([P, PLANES, GROUP], BF16)
+                h_planes_of[n] = h_planes_new
+            h_planes = h_planes_of[n]
+            for plane in range(first, behind):
                 bank = turned.tile([P, GROUP], F32)
                 for i in range(TILES):
                     nc.tensor.transpose(
@@ -276,7 +285,6 @@ def tile_minitransformerlayer_pa_t_kernel(
                     bias=bias[:, plane : plane + 1],
                     scale=gain[:, plane : plane + 1],
                 )
-            h_planes_of[n] = h_planes
 
         def quantise(n):
             if not 0 <= n < GROUPS:
@@ -337,13 +345,11 @@ def tile_minitransformerlayer_pa_t_kernel(
             sb = n % SEQ_BLOCKS
             acc_halves = acc_of[n][0]
             straight = work.tile([P, 2 * HEADS, TILES, D_HEAD], F32)
-            crossed = work.tile([P, 2 * HEADS, TILES, 2, D_HEAD // 2], F32)
+            crossed = work.tile([P, 2 * HEADS, TILES, D_HEAD], F32)
             shape_f = [P, 2, 2 * HEADS, D_HEAD]
-            shape_j = [P, 2, 2 * HEADS, D_HEAD // 2]
             for half in range(TILES // 2):
                 acc_qk = acc_halves[half]
                 two = slice(2 * half, 2 * half + 2)
-                pairs = acc_qk[:].rearrange("p ii (c j e) -> p ii c j e", c=2 * HEADS, e=2)
                 nc.vector.tensor_tensor(
                     out=straight[:, :, two, :].rearrange("p c ii f -> p ii c f"),
                     in0=acc_qk[:].rearrange("p ii (c f) -> p ii c f", c=2 * HEADS),
@@ -351,15 +357,14 @@ def tile_minitransformerlayer_pa_t_kernel(
                     op=ALU.mult,
                 )
                 nc.vector.tensor_tensor(
-                    out=crossed[:, :, two, 0, :].rearrange("p c ii j -> p ii c j"),
-                    in0=pairs[:, :, :, :, 1],
-                    in1=odd_minus[:, sb, two, :].unsqueeze(2).to_broadcast(shape_j),
-                    op=ALU.mult,
-                )
-                nc.vector.tensor_tensor(
-                    out=crossed[:, :, two, 1, :].rearrange("p c ii j -> p ii c j"),
-                    in0=pairs[:, :, :, :, 0],
-                    in1=odd_plus[:, sb, two, :].unsqueeze(2).to_broadcast(shape_j),
+                    out=crossed[:, :, two, :].rearrange("p c ii (j e) -> p ii c j e", e=2),
+                    in0=acc_qk[:].rearrange("p ii (c j e) -> p ii c j e", c=2 * HEADS, e=2)[
+                        :, :, :, :, ::-1
+                    ],
+                    in1=odd_signed[:, sb, two, :]
+                    .unsqueeze(2)
+                    .to_broadcast(shape_f)
+                    .rearrange("p ii c (j e) -> p ii c j e", e=2),
                     op=ALU.mult,
                 )
             products_of[n] = (straight, crossed)
@@ -378,9 +383,9 @@ def tile_minitransformerlayer_pa_t_kernel(
             )
             if n < GROUPS - 1:
                 nc.gpsimd.tensor_tensor(
-                    out=res[:, 0 : 2 * HEADS, :, :].rearrange("p c i (j e) -> p (c i) j e", e=2),
-                    in0=straight[:].rearrange("p c i (j e) -> p (c i) j e", e=2),
-                    in1=crossed[:].rearrange("p c i e j -> p (c i) j e"),
+                    out=res[:, 0 : 2 * HEADS, :, :].rearrange("p c i f -> p (c i f)"),
+                    in0=straight[:].rearrange("p c i f -> p (c i f)"),
+                    in1=crossed[:].rearrange("p c i f -> p (c i f)"),
                     op=ALU.add,
                 )
                 order = (0, 1, 2)
@@ -388,9 +393,9 @@ def tile_minitransformerlayer_pa_t_kernel(
                 for which in range(2):
                     heads = slice(which * HEADS, (which + 1) * HEADS)
                     nc.vector.tensor_tensor(
-                        out=res[:, heads, :, :].rearrange("p c i (j e) -> p (c i) j e", e=2),
-                        in0=straight[:, heads, :, :].rearrange("p c i (j e) -> p (c i) j e", e=2),
-                        in1=crossed[:, heads, :, :, :].rearrange("p c i e j -> p (c i) j e"),
+                        out=res[:, heads, :, :].rearrange("p c i f -> p (c i f)"),
+                        in0=straight[:, heads, :, :].rearrange("p c i f -> p (c i f)"),
+                        in1=crossed[:, heads, :, :].rearrange("p c i f -> p (c i f)"),
                         op=ALU.add,
                     )
                 order = (2, 0, 1)
@@ -412,8 +417,11 @@ def tile_minitransformerlayer_pa_t_kernel(
             reciprocals(t - 1)
             normalise_gpsimd(t - 1)
             combine_and_store(t - 5)
+            squares_scalar(t)
             project(t - 4)
             rotate_products(t - 4)
-            turn(t - 2)
+            turn(t - 2, 0, PLANES // 2)
+            shifts_scalar(t - 1)
+            turn(t - 2, PLANES // 2, PLANES)
             normalise_scalar(t - 1)
             statistics_vector(t)

@@ -54,7 +54,7 @@ def tile_minitransformerlayer_pa_t_kernel(
     ):
         x_of, mean_var_of, neg_mean_of, neg_mean_last_of, squares_of = {}, {}, {}, {}, {}
         std_of, rstd_of, normed_of, h_planes_of, h_words_of = {}, {}, {}, {}, {}
-        acc_of, products_of, shift_of = {}, {}, {}
+        acc_of, products_of, shift_of, grouped_of = {}, {}, {}, {}
 
         def load_tokens(n):
             if not 0 <= n < GROUPS:
@@ -286,12 +286,14 @@ def tile_minitransformerlayer_pa_t_kernel(
                     scale=gain[:, plane : plane + 1],
                 )
 
-        def quantise(n):
+        def regroup(n):
             if not 0 <= n < GROUPS:
                 return
             grouped = work.tile([P, PASSES, GROUP * PACK], BF16, align_bytes=64)
             h_codes = work.tile([P, PASSES, GROUP], U32, align_bytes=64)
             h_scales = work.tile([P, PASSES, GROUP], U8, align_bytes=64)
+            grouped_of[n] = grouped
+            h_words_of[n] = (h_codes, h_scales)
             for g in range(PASSES):
                 nc.vector.tensor_copy(
                     out=grouped[:, g, :].rearrange("p (c r j) -> p c j r", r=4, j=PACK),
@@ -299,11 +301,14 @@ def tile_minitransformerlayer_pa_t_kernel(
                         "p j (c r) -> p c j r", r=4
                     ),
                 )
-            for g in range(PASSES):
-                nc.vector.quantize_mx(
-                    out=h_codes[:, g, :].bitcast(FP8X4), scales=h_scales[:, g, :], in_=grouped[:, g, :]
-                )
-            h_words_of[n] = (h_codes, h_scales)
+
+        def quantise(n, g):
+            if not 0 <= n < GROUPS:
+                return
+            h_codes, h_scales = h_words_of[n]
+            nc.vector.quantize_mx(
+                out=h_codes[:, g, :].bitcast(FP8X4), scales=h_scales[:, g, :], in_=grouped_of[n][:, g, :]
+            )
 
         def project(n):
             if not 0 <= n < GROUPS:
@@ -413,10 +418,12 @@ def tile_minitransformerlayer_pa_t_kernel(
             load_tokens(t + 2)
             roots(t - 1)
             statistics_scalar(t)
-            quantise(t - 3)
+            regroup(t - 3)
+            quantise(t - 3, 0)
             reciprocals(t - 1)
-            normalise_gpsimd(t - 1)
+            quantise(t - 3, 1)
             combine_and_store(t - 5)
+            normalise_gpsimd(t - 1)
             squares_scalar(t)
             project(t - 4)
             rotate_products(t - 4)

@@ -214,14 +214,12 @@ def tile_minitransformerlayer_pa_t_kernel(
         def normalise_gpsimd(n):
             if not 0 <= n < GROUPS:
                 return
-            normed = work.tile([P, TILES, PLANES, P], F32)
+            normed = work.tile([P, TILES, D_MODEL], F32)
             for i in range(VECTOR_TILES):
                 passes = 1 if i == SHARED else PASSES
                 nc.gpsimd.tensor_scalar(
-                    out=normed[:, i, 0 : passes * PACK, :].rearrange("p (g j) q -> p g j q", j=PACK),
-                    in0=x_of[n][:, i, 0 : passes * K_PASS].rearrange(
-                        "p (g q j) -> p g j q", g=passes, j=PACK
-                    ),
+                    out=normed[:, i, 0 : passes * K_PASS],
+                    in0=x_of[n][:, i, 0 : passes * K_PASS],
                     scalar1=neg_mean_of[n][:, i : i + 1],
                     scalar2=rstd_of[n][:, i : i + 1],
                     op0=ALU.add,
@@ -249,15 +247,15 @@ def tile_minitransformerlayer_pa_t_kernel(
                 return
             shift_last, shift_shared = shift_of[n]
             nc.scalar.activation(
-                out=normed_of[n][:, SHARED, PACK:PLANES, :],
-                in_=x_of[n][:, SHARED, K_PASS:D_MODEL].rearrange("p (q j) -> p j q", j=PACK),
+                out=normed_of[n][:, SHARED, K_PASS:D_MODEL],
+                in_=x_of[n][:, SHARED, K_PASS:D_MODEL],
                 func=ACT.Identity,
                 bias=shift_shared[:],
                 scale=rstd_of[n][:, SHARED : SHARED + 1],
             )
             nc.scalar.activation(
-                out=normed_of[n][:, last, :, :].rearrange("p (g j) q -> p g j q", j=PACK),
-                in_=x_of[n][:, last, :].rearrange("p (g q j) -> p g j q", g=PASSES, j=PACK),
+                out=normed_of[n][:, last, :],
+                in_=x_of[n][:, last, :],
                 func=ACT.Identity,
                 bias=shift_last[:],
                 scale=rstd_of[n][:, last:TILES],
@@ -275,7 +273,9 @@ def tile_minitransformerlayer_pa_t_kernel(
                 for i in range(TILES):
                     nc.tensor.transpose(
                         out=bank[:, i * P : (i + 1) * P],
-                        in_=normed_of[n][:, i, plane, :],
+                        in_=normed_of[n][:, i, :].rearrange("p (g q j) -> p g j q", g=PASSES, j=PACK)[
+                            :, plane // PACK, plane % PACK, :
+                        ],
                         identity=ident[:],
                     )
                 nc.scalar.activation(

@@ -215,9 +215,10 @@ def tile_minitransformerlayer_pa_t_kernel(
             if not 0 <= n < GROUPS:
                 return
             normed = work.tile([P, TILES, D_MODEL], F32)
+            engine = nc.vector if n == 0 else nc.gpsimd
             for i in range(VECTOR_TILES):
                 passes = 1 if i == SHARED else PASSES
-                nc.gpsimd.tensor_scalar(
+                engine.tensor_scalar(
                     out=normed[:, i, 0 : passes * K_PASS],
                     in0=x_of[n][:, i, 0 : passes * K_PASS],
                     scalar1=neg_mean_of[n][:, i : i + 1],

@@ -28,6 +28,7 @@ GROUPS = BATCH * SEQ // GROUP
 SEQ_BLOCKS = SEQ // GROUP
 BN_CHUNK = 512
 VECTOR_TILES = TILES - 1
+SCALAR_TOKENS = 128
 SHARED = VECTOR_TILES - 1
 
 FLOPS = 2 * BATCH * SEQ * D_MODEL * N_OUT
@@ -47,7 +48,8 @@ def tile_minitransformerlayer_pa_t_kernel(
         tc.tile_pool(name="small", bufs=4) as small,
         tc.tile_pool(name="work", bufs=2) as work,
         tc.tile_pool(name="result", bufs=2) as result,
-        tc.psum_pool(name="turned", bufs=4) as turned,
+        tc.psum_pool(name="turned", bufs=3) as turned,
+        tc.psum_pool(name="folded", bufs=1) as folded,
         tc.psum_pool(name="prod_qk", bufs=2) as prod_qk,
         tc.psum_pool(name="prod_v", bufs=2) as prod_v,
         tc.manual_schedule(),
@@ -55,6 +57,7 @@ def tile_minitransformerlayer_pa_t_kernel(
         x_of, mean_var_of, neg_mean_of, neg_mean_last_of, squares_of = {}, {}, {}, {}, {}
         std_of, rstd_of, normed_of, h_planes_of, h_words_of = {}, {}, {}, {}, {}
         acc_of, products_of, shift_of, grouped_of = {}, {}, {}, {}
+        sum_of = {}
 
         def load_tokens(n):
             if not 0 <= n < GROUPS:
@@ -81,6 +84,8 @@ def tile_minitransformerlayer_pa_t_kernel(
         nc.scalar.activation(out=sqrt_first[:], in_=eps_col[:], func=ACT.Sqrt)
         ident = const.tile([P, P], F32)
         make_identity(nc, ident[:])
+        ident_bf = const.tile([P, P], BF16)
+        make_identity(nc, ident_bf[:])
 
         w_codes = const.tile([P, PASSES, N_OUT], U32, align_bytes=64)
         nc.sync.dma_start(
@@ -149,15 +154,29 @@ def tile_minitransformerlayer_pa_t_kernel(
                 )
             mean_var_of[n] = mean_var
 
+        def fold_tensor(n):
+            if not 0 <= n < GROUPS:
+                return
+            sums = folded.tile([P, P], F32)
+            blocks = D_MODEL // P
+            for m in range(blocks):
+                nc.tensor.matmul(
+                    out=sums[:],
+                    lhsT=ident_bf[:],
+                    rhs=x_of[n][:, last, m * P : (m + 1) * P],
+                    start=(m == 0),
+                    stop=(m == blocks - 1),
+                )
+            sum_of[n] = sums
+
         def statistics_scalar(n):
             if not 0 <= n < GROUPS:
                 return
-            x_sb = x_of[n]
-            unread_a = work.tile([P, D_MODEL], BF16)
+            unread_a = work.tile([P, P], BF16)
             neg_mean_last = small.tile([P, 1], F32)
             nc.scalar.activation(
                 out=unread_a[:],
-                in_=x_sb[:, last, :],
+                in_=sum_of[n][:],
                 func=ACT.Identity,
                 scale=-1.0 / D_MODEL,
                 accum_out=neg_mean_last[:],
@@ -287,21 +306,29 @@ def tile_minitransformerlayer_pa_t_kernel(
                     scale=gain[:, plane : plane + 1],
                 )
 
-        def regroup(n):
+        def regroup_views(n, g, first, behind):
+            return (
+                grouped_of[n][:, g, first * PACK : behind * PACK].rearrange("p (c r j) -> p c j r", r=4, j=PACK),
+                h_planes_of[n][:, g * PACK : (g + 1) * PACK, first:behind].rearrange("p j (c r) -> p c j r", r=4),
+            )
+
+        def regroup_scalar(n):
             if not 0 <= n < GROUPS:
                 return
             grouped = work.tile([P, PASSES, GROUP * PACK], BF16, align_bytes=64)
+            grouped_of[n] = grouped
+            side_by_side, planes = regroup_views(n, PASSES - 1, GROUP - SCALAR_TOKENS, GROUP)
+            nc.scalar.copy(out=side_by_side, in_=planes)
+
+        def regroup(n):
+            if not 0 <= n < GROUPS:
+                return
             h_codes = work.tile([P, PASSES, GROUP], U32, align_bytes=64)
             h_scales = work.tile([P, PASSES, GROUP], U8, align_bytes=64)
-            grouped_of[n] = grouped
             h_words_of[n] = (h_codes, h_scales)
             for g in range(PASSES):
-                nc.vector.tensor_copy(
-                    out=grouped[:, g, :].rearrange("p (c r j) -> p c j r", r=4, j=PACK),
-                    in_=h_planes_of[n][:, g * PACK : (g + 1) * PACK, :].rearrange(
-                        "p j (c r) -> p c j r", r=4
-                    ),
-                )
+                side_by_side, planes = regroup_views(n, g, 0, GROUP if g < PASSES - 1 else GROUP - SCALAR_TOKENS)
+                nc.vector.tensor_copy(out=side_by_side, in_=planes)
 
         def quantise(n, g):
             if not 0 <= n < GROUPS:
@@ -415,6 +442,7 @@ def tile_minitransformerlayer_pa_t_kernel(
                     ),
                 )
 
+        fold_tensor(0)
         for t in range(GROUPS + 5):
             load_tokens(t + 2)
             roots(t - 1)
@@ -431,5 +459,7 @@ def tile_minitransformerlayer_pa_t_kernel(
             turn(t - 2, 0, PLANES // 2)
             shifts_scalar(t - 1)
             turn(t - 2, PLANES // 2, PLANES)
+            fold_tensor(t + 1)
             normalise_scalar(t - 1)
+            regroup_scalar(t - 2)
             statistics_vector(t)

@@ -48,8 +48,7 @@ def tile_minitransformerlayer_pa_t_kernel(
         tc.tile_pool(name="small", bufs=4) as small,
         tc.tile_pool(name="work", bufs=2) as work,
         tc.tile_pool(name="result", bufs=2) as result,
-        tc.psum_pool(name="turned", bufs=3) as turned,
-        tc.psum_pool(name="folded", bufs=1) as folded,
+        tc.psum_pool(name="turned", bufs=4) as turned,
         tc.psum_pool(name="prod_qk", bufs=2) as prod_qk,
         tc.psum_pool(name="prod_v", bufs=2) as prod_v,
         tc.manual_schedule(),
@@ -157,17 +156,17 @@ def tile_minitransformerlayer_pa_t_kernel(
         def fold_tensor(n):
             if not 0 <= n < GROUPS:
                 return
-            sums = folded.tile([P, P], F32)
+            bank = turned.tile([P, P], F32)
             blocks = D_MODEL // P
             for m in range(blocks):
                 nc.tensor.matmul(
-                    out=sums[:],
+                    out=bank[:],
                     lhsT=ident_bf[:],
                     rhs=x_of[n][:, last, m * P : (m + 1) * P],
                     start=(m == 0),
                     stop=(m == blocks - 1),
                 )
-            sum_of[n] = sums
+            sum_of[n] = bank
 
         def statistics_scalar(n):
             if not 0 <= n < GROUPS:
@@ -317,8 +316,11 @@ def tile_minitransformerlayer_pa_t_kernel(
                 return
             grouped = work.tile([P, PASSES, GROUP * PACK], BF16, align_bytes=64)
             grouped_of[n] = grouped
-            side_by_side, planes = regroup_views(n, PASSES - 1, GROUP - SCALAR_TOKENS, GROUP)
-            nc.scalar.copy(out=side_by_side, in_=planes)
+            first = GROUP - SCALAR_TOKENS
+            nc.scalar.copy(
+                out=grouped[:, PASSES - 1, first * PACK : GROUP * PACK].rearrange("p (c j) -> p c j", j=PACK),
+                in_=h_planes_of[n][:, (PASSES - 1) * PACK : PLANES, first:GROUP].rearrange("p j c -> p c j"),
+            )
 
         def regroup(n):
             if not 0 <= n < GROUPS:

@@ -29,6 +29,7 @@ SEQ_BLOCKS = SEQ // GROUP
 BN_CHUNK = 512
 VECTOR_TILES = TILES - 1
 SCALAR_TOKENS = 128
+HELPED = 1
 SHARED = VECTOR_TILES - 1
 
 FLOPS = 2 * BATCH * SEQ * D_MODEL * N_OUT
@@ -247,7 +248,7 @@ def tile_minitransformerlayer_pa_t_kernel(
             normed_of[n] = normed
 
         def shifts_scalar(n):
-            if not 0 <= n < GROUPS:
+            if not 0 <= n < GROUPS or n == HELPED:
                 return
             shift_last = small.tile([P, 1], F32)
             shift_shared = small.tile([P, 1], F32)
@@ -263,6 +264,20 @@ def tile_minitransformerlayer_pa_t_kernel(
 
         def normalise_scalar(n):
             if not 0 <= n < GROUPS:
+                return
+            if n == HELPED:
+                for i, first, neg_mean in (
+                    (SHARED, K_PASS, neg_mean_of[n][:, SHARED : SHARED + 1]),
+                    (last, 0, neg_mean_last_of[n][:]),
+                ):
+                    nc.vector.tensor_scalar(
+                        out=normed_of[n][:, i, first:D_MODEL],
+                        in0=x_of[n][:, i, first:D_MODEL],
+                        scalar1=neg_mean,
+                        scalar2=rstd_of[n][:, i : i + 1],
+                        op0=ALU.add,
+                        op1=ALU.mult,
+                    )
                 return
             shift_last, shift_shared = shift_of[n]
             nc.scalar.activation(

@@ -28,7 +28,7 @@ GROUPS = BATCH * SEQ // GROUP
 SEQ_BLOCKS = SEQ // GROUP
 BN_CHUNK = 512
 VECTOR_TILES = TILES - 1
-SCALAR_TOKENS = 128
+SCALAR_TOKENS = 160
 HELPED = 1
 SHARED = VECTOR_TILES - 1
 
@@ -219,13 +219,13 @@ def tile_minitransformerlayer_pa_t_kernel(
                 scale=1.0 / D_MODEL,
             )
             std_of[n] = std
+            neg_mean = small.tile([P, VECTOR_TILES], F32)
+            nc.scalar.mul(out=neg_mean[:], in_=mean_var_of[n][:, :, 0], mul=-1.0)
+            neg_mean_of[n] = neg_mean
 
         def reciprocals(n):
             if not 0 <= n < GROUPS:
                 return
-            neg_mean = small.tile([P, VECTOR_TILES], F32)
-            nc.vector.tensor_scalar_mul(out=neg_mean[:], in0=mean_var_of[n][:, :, 0], scalar1=-1.0)
-            neg_mean_of[n] = neg_mean
             rstd = small.tile([P, TILES], F32)
             nc.vector.reciprocal(out=rstd[:], in_=std_of[n][:])
             rstd_of[n] = rstd

from concourse import mybir
from concourse.masks import make_identity

F32 = mybir.dt.float32
BF16 = mybir.dt.bfloat16
I32 = mybir.dt.int32
U32 = mybir.dt.uint32
U8 = mybir.dt.uint8
FP8X4 = mybir.dt.float8_e4m3fn_x4
ACT = mybir.ActivationFunctionType
ALU = mybir.AluOpType

P = 128
PACK = 4
K_PASS = P * PACK

BATCH, SEQ, D_MODEL, HEADS, D_HEAD = 4, 2048, 1024, 2, 64
N_QK = 2 * HEADS * D_HEAD
N_V = HEADS * D_HEAD
N_OUT = N_QK + N_V
PASSES = D_MODEL // K_PASS
PLANES = PASSES * PACK
EPS = 1e-5

TILES = 4
GROUP = TILES * P
GROUPS = BATCH * SEQ // GROUP
SEQ_BLOCKS = SEQ // GROUP
BN_CHUNK = 512
VECTOR_TILES = TILES - 1
SCALAR_TOKENS = 160
HELPED = 1
SHARED = VECTOR_TILES - 1

FLOPS = 2 * BATCH * SEQ * D_MODEL * N_OUT


def tile_minitransformerlayer_pa_t_kernel(
    tc, x, pe, w_qkv_words, w_qkv_scales, g1, b1, out_0, out_1, out_2
):
    nc = tc.nc
    x_rows = x.flatten_outer_dims()
    outs = (out_0, out_1, out_2)
    last = VECTOR_TILES

    with (
        tc.tile_pool(name="const", bufs=1) as const,
        tc.tile_pool(name="load", bufs=4) as load,
        tc.tile_pool(name="small", bufs=4) as small,
        tc.tile_pool(name="work", bufs=2) as work,
        tc.tile_pool(name="result", bufs=2) as result,
        tc.psum_pool(name="turned", bufs=4) as turned,
        tc.psum_pool(name="prod_qk", bufs=2) as prod_qk,
        tc.psum_pool(name="prod_v", bufs=2) as prod_v,
        tc.manual_schedule(),
    ):
        x_of, mean_var_of, neg_mean_of, neg_mean_last_of, squares_of = {}, {}, {}, {}, {}
        std_of, rstd_of, normed_of, h_planes_of, h_words_of = {}, {}, {}, {}, {}
        acc_of, products_of, shift_of, grouped_of = {}, {}, {}, {}
        sum_of = {}

        def load_tokens(n):
            if not 0 <= n < GROUPS:
                return
            x_sb = load.tile([P, TILES, D_MODEL], BF16)
            rows = x_rows[n * GROUP : (n + 1) * GROUP, :]
            if n == 0:
                by_tile = rows.rearrange("(p i) k -> p i k", i=TILES)
                for i in (0, last, 1, 2):
                    nc.sync.dma_start(out=x_sb[:, i, :], in_=by_tile[:, i, :])
            else:
                nc.sync.dma_start(
                    out=x_sb[:].rearrange("p i k -> p (i k)"),
                    in_=rows.rearrange("(p i) k -> p (i k)", i=TILES),
                )
            x_of[n] = x_sb

        load_tokens(0)
        load_tokens(1)

        eps_col = const.tile([P, 1], F32)
        nc.vector.memset(eps_col[:], EPS)
        sqrt_first = const.tile([P, 1], F32)
        nc.scalar.activation(out=sqrt_first[:], in_=eps_col[:], func=ACT.Sqrt)
        ident = const.tile([P, P], F32)
        make_identity(nc, ident[:])
        ident_bf = const.tile([P, P], BF16)
        make_identity(nc, ident_bf[:])

        w_codes = const.tile([P, PASSES, N_OUT], U32, align_bytes=64)
        nc.sync.dma_start(
            out=w_codes[:].bitcast(I32),
            in_=w_qkv_words.rearrange("g p n t -> p g (n t)").bitcast(I32),
        )
        w_planes = const.tile([P, PASSES, N_OUT], U8, align_bytes=64)
        nc.vector.memset(w_planes[:].bitcast(I32), 0)
        for quad in range(4):
            nc.sync.dma_start(
                out=w_planes[32 * quad : 32 * quad + 4, :, :].bitcast(I32),
                in_=w_qkv_scales[:, 4 * quad : 4 * quad + 4, :]
                .rearrange("g r n -> r g n")
                .bitcast(I32),
            )

        gain_bf = const.tile([P, PASSES, PACK], BF16)
        bias_bf = const.tile([P, PASSES, PACK], BF16)
        nc.sync.dma_start(out=gain_bf[:], in_=g1.rearrange("(g q j) -> q g j", g=PASSES, j=PACK))
        nc.sync.dma_start(out=bias_bf[:], in_=b1.rearrange("(g q j) -> q g j", g=PASSES, j=PACK))
        gain = const.tile([P, PLANES], F32)
        bias = const.tile([P, PLANES], F32)
        nc.gpsimd.tensor_copy(out=gain[:], in_=gain_bf[:].rearrange("q g j -> q (g j)"))
        nc.gpsimd.tensor_copy(out=bias[:], in_=bias_bf[:].rearrange("q g j -> q (g j)"))

        pe_bf = const.tile([P, SEQ_BLOCKS, TILES * D_HEAD], BF16)
        nc.sync.dma_start(
            out=pe_bf[:], in_=pe.rearrange("(sb p i) f -> p sb (i f)", sb=SEQ_BLOCKS, i=TILES)
        )
        pe_pairs = pe_bf[:].rearrange("p sb (n e) -> p (sb n) e", e=2)
        n_pairs = SEQ_BLOCKS * TILES * D_HEAD // 2
        even_twice = const.tile([P, SEQ_BLOCKS, TILES, D_HEAD], F32)
        odd_signed = const.tile([P, SEQ_BLOCKS, TILES, D_HEAD], F32)
        nc.gpsimd.tensor_scalar(
            out=even_twice[:].rearrange("p sb i (j e) -> p (sb i j) e", e=2),
            in0=pe_pairs[:, :, 0].unsqueeze(2).to_broadcast([P, n_pairs, 2]),
            scalar1=1.0,
            scalar2=0.0,
            op0=ALU.mult,
            op1=ALU.add,
        )
        for e, sign in ((0, -1.0), (1, 1.0)):
            nc.gpsimd.tensor_scalar(
                out=odd_signed[:].rearrange("p sb i (j e) -> p (sb i j) e", e=2)[:, :, e],
                in0=pe_pairs[:, :, 1],
                scalar1=sign,
                scalar2=0.0,
                op0=ALU.mult,
                op1=ALU.add,
            )

        def statistics_vector(n):
            if not 0 <= n < GROUPS:
                return
            x_sb = x_of[n]
            stats = small.tile([P, VECTOR_TILES, D_MODEL // BN_CHUNK, 6], F32)
            mean_var = small.tile([P, VECTOR_TILES, 2], F32)
            for i in range(VECTOR_TILES):
                for c in range(D_MODEL // BN_CHUNK):
                    nc.vector.bn_stats(
                        out=stats[:, i, c, :], in_=x_sb[:, i, c * BN_CHUNK : (c + 1) * BN_CHUNK]
                    )
            for i in range(VECTOR_TILES):
                nc.vector.bn_aggr(
                    out=mean_var[:, i, :], in_=stats[:, i, :, :].rearrange("p c s -> p (c s)")
                )
            mean_var_of[n] = mean_var

        def fold_tensor(n):
            if not 0 <= n < GROUPS:
                return
            bank = turned.tile([P, P], F32)
            blocks = D_MODEL // P
            for m in range(blocks):
                nc.tensor.matmul(
                    out=bank[:],
                    lhsT=ident_bf[:],
                    rhs=x_of[n][:, last, m * P : (m + 1) * P],
                    start=(m == 0),
                    stop=(m == blocks - 1),
                )
            sum_of[n] = bank

        def statistics_scalar(n):
            if not 0 <= n < GROUPS:
                return
            unread_a = work.tile([P, P], BF16)
            neg_mean_last = small.tile([P, 1], F32)
            nc.scalar.activation(
                out=unread_a[:],
                in_=sum_of[n][:],
                func=ACT.Identity,
                scale=-1.0 / D_MODEL,
                accum_out=neg_mean_last[:],
            )
            neg_mean_last_of[n] = neg_mean_last

        def squares_scalar(n):
            if not 0 <= n < GROUPS:
                return
            x_sb = x_of[n]
            neg_mean_last = neg_mean_last_of[n]
            unread_b = work.tile([P, D_MODEL], BF16)
            squares = small.tile([P, 1], F32)
            nc.scalar.activation(
                out=unread_b[:],
                in_=x_sb[:, last, :],
                func=ACT.Square,
                bias=neg_mean_last[:],
                scale=1.0,
                accum_out=squares[:],
            )
            squares_of[n] = squares

        def roots(n):
            if not 0 <= n < GROUPS:
                return
            std = small.tile([P, TILES], F32)
            nc.scalar.activation(
                out=std[:, 0:last],
                in_=mean_var_of[n][:, :, 1],
                func=ACT.Sqrt,
                bias=eps_col[:],
                scale=1.0,
            )
            nc.scalar.activation(
                out=std[:, last:TILES],
                in_=squares_of[n][:],
                func=ACT.Sqrt,
                bias=eps_col[:],
                scale=1.0 / D_MODEL,
            )
            std_of[n] = std
            neg_mean = small.tile([P, VECTOR_TILES], F32)
            nc.scalar.mul(out=neg_mean[:], in_=mean_var_of[n][:, :, 0], mul=-1.0)
            neg_mean_of[n] = neg_mean

        def reciprocals(n):
            if not 0 <= n < GROUPS:
                return
            rstd = small.tile([P, TILES], F32)
            nc.vector.reciprocal(out=rstd[:], in_=std_of[n][:])
            rstd_of[n] = rstd

        def normalise_gpsimd(n):
            if not 0 <= n < GROUPS:
                return
            normed = work.tile([P, TILES, D_MODEL], F32)
            engine = nc.vector if n == 0 else nc.gpsimd
            for i in range(VECTOR_TILES):
                passes = 1 if i == SHARED else PASSES
                engine.tensor_scalar(
                    out=normed[:, i, 0 : passes * K_PASS],
                    in0=x_of[n][:, i, 0 : passes * K_PASS],
                    scalar1=neg_mean_of[n][:, i : i + 1],
                    scalar2=rstd_of[n][:, i : i + 1],
                    op0=ALU.add,
                    op1=ALU.mult,
                )
            normed_of[n] = normed

        def shifts_scalar(n):
            if not 0 <= n < GROUPS or n == HELPED:
                return
            shift_last = small.tile([P, 1], F32)
            shift_shared = small.tile([P, 1], F32)
            nc.scalar.mul(
                out=shift_last[:], in_=neg_mean_last_of[n][:], mul=rstd_of[n][:, last:TILES]
            )
            nc.scalar.mul(
                out=shift_shared[:],
                in_=neg_mean_of[n][:, SHARED : SHARED + 1],
                mul=rstd_of[n][:, SHARED : SHARED + 1],
            )
            shift_of[n] = (shift_last, shift_shared)

        def normalise_scalar(n):
            if not 0 <= n < GROUPS:
                return
            if n == HELPED:
                for i, first, neg_mean in (
                    (SHARED, K_PASS, neg_mean_of[n][:, SHARED : SHARED + 1]),
                    (last, 0, neg_mean_last_of[n][:]),
                ):
                    nc.vector.tensor_scalar(
                        out=normed_of[n][:, i, first:D_MODEL],
                        in0=x_of[n][:, i, first:D_MODEL],
                        scalar1=neg_mean,
                        scalar2=rstd_of[n][:, i : i + 1],
                        op0=ALU.add,
                        op1=ALU.mult,
                    )
                return
            shift_last, shift_shared = shift_of[n]
            nc.scalar.activation(
                out=normed_of[n][:, SHARED, K_PASS:D_MODEL],
                in_=x_of[n][:, SHARED, K_PASS:D_MODEL],
                func=ACT.Identity,
                bias=shift_shared[:],
                scale=rstd_of[n][:, SHARED : SHARED + 1],
            )
            nc.scalar.activation(
                out=normed_of[n][:, last, :],
                in_=x_of[n][:, last, :],
                func=ACT.Identity,
                bias=shift_last[:],
                scale=rstd_of[n][:, last:TILES],
            )

        def turn(n, first, behind):
            if not 0 <= n < GROUPS:
                return
            if first == 0:
                h_planes_new = work.tile([P, PLANES, GROUP], BF16)
                h_planes_of[n] = h_planes_new
            h_planes = h_planes_of[n]
            for plane in range(first, behind):
                bank = turned.tile([P, GROUP], F32)
                for i in range(TILES):
                    nc.tensor.transpose(
                        out=bank[:, i * P : (i + 1) * P],
                        in_=normed_of[n][:, i, :].rearrange("p (g q j) -> p g j q", g=PASSES, j=PACK)[
                            :, plane // PACK, plane % PACK, :
                        ],
                        identity=ident[:],
                    )
                nc.scalar.activation(
                    out=h_planes[:, plane, :],
                    in_=bank[:],
                    func=ACT.Identity,
                    bias=bias[:, plane : plane + 1],
                    scale=gain[:, plane : plane + 1],
                )

        def regroup_views(n, g, first, behind):
            return (
                grouped_of[n][:, g, first * PACK : behind * PACK].rearrange("p (c r j) -> p c j r", r=4, j=PACK),
                h_planes_of[n][:, g * PACK : (g + 1) * PACK, first:behind].rearrange("p j (c r) -> p c j r", r=4),
            )

        def regroup_scalar(n):
            if not 0 <= n < GROUPS:
                return
            grouped = work.tile([P, PASSES, GROUP * PACK], BF16, align_bytes=64)
            grouped_of[n] = grouped
            first = GROUP - SCALAR_TOKENS
            nc.scalar.copy(
                out=grouped[:, PASSES - 1, first * PACK : GROUP * PACK].rearrange("p (c j) -> p c j", j=PACK),
                in_=h_planes_of[n][:, (PASSES - 1) * PACK : PLANES, first:GROUP].rearrange("p j c -> p c j"),
            )

        def regroup(n):
            if not 0 <= n < GROUPS:
                return
            h_codes = work.tile([P, PASSES, GROUP], U32, align_bytes=64)
            h_scales = work.tile([P, PASSES, GROUP], U8, align_bytes=64)
            h_words_of[n] = (h_codes, h_scales)
            for g in range(PASSES):
                side_by_side, planes = regroup_views(n, g, 0, GROUP if g < PASSES - 1 else GROUP - SCALAR_TOKENS)
                nc.vector.tensor_copy(out=side_by_side, in_=planes)

        def quantise(n, g):
            if not 0 <= n < GROUPS:
                return
            h_codes, h_scales = h_words_of[n]
            nc.vector.quantize_mx(
                out=h_codes[:, g, :].bitcast(FP8X4), scales=h_scales[:, g, :], in_=grouped_of[n][:, g, :]
            )

        def project(n):
            if not 0 <= n < GROUPS:
                return
            h_codes, h_scales = h_words_of[n]
            acc_v = prod_v.tile([P, TILES, N_V], F32)
            acc_halves = []
            for half in range(TILES // 2):
                acc_qk = prod_qk.tile([P, 2, N_QK], F32)
                acc_halves.append(acc_qk)
                for ii in range(2):
                    i = 2 * half + ii
                    toks = slice(i * P, (i + 1) * P)
                    for g in range(PASSES):
                        nc.tensor.matmul_mx(
                            out=acc_qk[:, ii, :],
                            lhsT=h_codes[:, g, toks].bitcast(FP8X4),
                            lhsT_scale=h_scales[:, g, toks],
                            rhs=w_codes[:, g, 0:N_QK].bitcast(FP8X4),
                            rhs_scale=w_planes[:, g, 0:N_QK],
                            start=(g == 0),
                            stop=(g == PASSES - 1),
                        )
                    for g in range(PASSES):
                        nc.tensor.matmul_mx(
                            out=acc_v[:, i, :],
                            lhsT=h_codes[:, g, toks].bitcast(FP8X4),
                            lhsT_scale=h_scales[:, g, toks],
                            rhs=w_codes[:, g, N_QK:N_OUT].bitcast(FP8X4),
                            rhs_scale=w_planes[:, g, N_QK:N_OUT],
                            start=(g == 0),
                            stop=(g == PASSES - 1),
                        )
            acc_of[n] = (acc_halves, acc_v)

        def rotate_products(n):
            if not 0 <= n < GROUPS:
                return
            sb = n % SEQ_BLOCKS
            acc_halves = acc_of[n][0]
            straight = work.tile([P, 2 * HEADS, TILES, D_HEAD], F32)
            crossed = work.tile([P, 2 * HEADS, TILES, D_HEAD], F32)
            shape_f = [P, 2, 2 * HEADS, D_HEAD]
            for half in range(TILES // 2):
                acc_qk = acc_halves[half]
                two = slice(2 * half, 2 * half + 2)
                nc.vector.tensor_tensor(
                    out=straight[:, :, two, :].rearrange("p c ii f -> p ii c f"),
                    in0=acc_qk[:].rearrange("p ii (c f) -> p ii c f", c=2 * HEADS),
                    in1=even_twice[:, sb, two, :].unsqueeze(2).to_broadcast(shape_f),
                    op=ALU.mult,
                )
                nc.vector.tensor_tensor(
                    out=crossed[:, :, two, :].rearrange("p c ii (j e) -> p ii c j e", e=2),
                    in0=acc_qk[:].rearrange("p ii (c j e) -> p ii c j e", c=2 * HEADS, e=2)[
                        :, :, :, :, ::-1
                    ],
                    in1=odd_signed[:, sb, two, :]
                    .unsqueeze(2)
                    .to_broadcast(shape_f)
                    .rearrange("p ii c (j e) -> p ii c j e", e=2),
                    op=ALU.mult,
                )
            products_of[n] = (straight, crossed)

        def combine_and_store(n):
            if not 0 <= n < GROUPS:
                return
            batch, sb = divmod(n, SEQ_BLOCKS)
            positions = slice(sb * GROUP, (sb + 1) * GROUP)
            straight, crossed = products_of[n]
            acc_v = acc_of[n][1]
            res = result.tile([P, 3 * HEADS, TILES, D_HEAD], F32)
            nc.scalar.copy(
                out=res[:, 2 * HEADS : 3 * HEADS, :, :].rearrange("p h i f -> p i h f"),
                in_=acc_v[:].rearrange("p i (h f) -> p i h f", h=HEADS),
            )
            if n < GROUPS - 1:
                nc.gpsimd.tensor_tensor(
                    out=res[:, 0 : 2 * HEADS, :, :].rearrange("p c i f -> p (c i f)"),
                    in0=straight[:].rearrange("p c i f -> p (c i f)"),
                    in1=crossed[:].rearrange("p c i f -> p (c i f)"),
                    op=ALU.add,
                )
                order = (0, 1, 2)
            else:
                for which in range(2):
                    heads = slice(which * HEADS, (which + 1) * HEADS)
                    nc.vector.tensor_tensor(
                        out=res[:, heads, :, :].rearrange("p c i f -> p (c i f)"),
                        in0=straight[:, heads, :, :].rearrange("p c i f -> p (c i f)"),
                        in1=crossed[:, heads, :, :].rearrange("p c i f -> p (c i f)"),
                        op=ALU.add,
                    )
                order = (2, 0, 1)
            for which in order:
                nc.sync.dma_start(
                    out=outs[which][batch, :, positions, :].rearrange(
                        "h (p i) f -> p h (i f)", i=TILES
                    ),
                    in_=res[:, which * HEADS : (which + 1) * HEADS, :, :].rearrange(
                        "p h i f -> p h (i f)"
                    ),
                )

        fold_tensor(0)
        for t in range(GROUPS + 5):
            load_tokens(t + 2)
            roots(t - 1)
            statistics_scalar(t)
            regroup(t - 3)
            quantise(t - 3, 0)
            reciprocals(t - 1)
            quantise(t - 3, 1)
            combine_and_store(t - 5)
            normalise_gpsimd(t - 1)
            squares_scalar(t)
            project(t - 4)
            rotate_products(t - 4)
            turn(t - 2, 0, PLANES // 2)
            shifts_scalar(t - 1)
            turn(t - 2, PLANES // 2, PLANES)
            fold_tensor(t + 1)
            normalise_scalar(t - 1)
            regroup_scalar(t - 2)
            statistics_vector(t)
